import numpy as np
import ml_dtypes


def mxq(x, axis, fmt="e4m3"):
    dtype, down = {"e4m3": (ml_dtypes.float8_e4m3fn, 7), "e5m2": (ml_dtypes.float8_e5m2, 14)}[fmt]
    v = np.moveaxis(np.asarray(x, np.float32).astype(ml_dtypes.bfloat16).astype(np.float64), axis, -1)
    blocks = v.reshape(v.shape[:-1] + (-1, 32))
    amax = np.abs(blocks).max(-1, keepdims=True)
    byte = np.maximum(np.where(amax > 0, np.frexp(amax)[1] - 1 + 127, 0) - down, 1)
    scale = np.exp2(byte - 127.0)
    codes = (blocks / scale).astype(np.float32).astype(dtype).astype(np.float64)
    return np.moveaxis((codes * scale).reshape(v.shape), -1, axis)


WIDE = False


def mx_kscale(k):
    if not WIDE:
        return np.ones(k)
    levels = np.array([10, -10, 5, -5, 0])
    a = np.random.permutation(np.resize(levels, k // 512 * 4)).reshape(k // 512, 4)
    idx = np.arange(k)
    return np.exp2(a[idx // 512, idx % 128 // 32])


BF16 = ml_dtypes.bfloat16


def bf(x):
    return np.asarray(x, np.float32).astype(BF16)


def f64(x):
    return np.asarray(x).astype(np.float64)


E2M1 = np.array([0.0, 0.5, 1.0, 1.5, 2.0, 3.0, 4.0, 6.0, -0.0, -0.5, -1.0, -1.5, -2.0, -3.0, -4.0, -6.0])


def pack_weight(w, fmt):
    k, n = w.shape
    w = f64(bf(w)).reshape(k // 32, 32, n)
    amax = np.abs(w).max(1)
    if fmt == "e4m3":
        byte = np.frexp(amax)[1] - 1 + 127 - 7
    else:
        mant, ex = np.frexp(amax / 6.0)
        byte = np.where(mant > 0.5, ex, ex - 1) + 127
    byte = np.clip(np.where(amax > 0, byte, 1), 1, 254)
    scaled = (w * np.exp2(127.0 - byte)[:, None, :]).reshape(k, n).astype(np.float32)
    by_word = np.ascontiguousarray(scaled.reshape(k // 512, 128, 4, n).transpose(0, 1, 3, 2))
    if fmt == "e4m3":
        words = by_word.astype(ml_dtypes.float8_e4m3fn).view(np.uint8)
    else:
        c = by_word.astype(ml_dtypes.float4_e2m1fn).view(np.uint8) & 0xF
        words = c[..., 0::2] | (c[..., 1::2] << 4)
    return np.ascontiguousarray(words), np.ascontiguousarray(byte.astype(np.uint8).reshape(k // 512, 16, n))


def unpack_weight(words, scales, fmt):
    g, p, n, _ = words.shape
    if fmt == "e4m3":
        vals = np.ascontiguousarray(words).view(ml_dtypes.float8_e4m3fn).astype(np.float64)
    else:
        nib = np.empty((g, p, n, 4), np.uint8)
        nib[..., 0::2] = words & 0xF
        nib[..., 1::2] = words >> 4
        vals = E2M1[nib]
    vals = vals * np.repeat(np.exp2(scales.astype(np.float64) - 127.0), 8, axis=1)[..., None]
    return vals.transpose(0, 1, 3, 2).reshape(g * 512, n)


N, MI, MO, LMAX = 16, 2048, 2048, 3
C = (LMAX + 1) ** 2
FMT = "e4m3"


def setup_inputs():
    s = mx_kscale(MI)
    d = {"x": bf(np.random.standard_normal((N, MI, C)) * s[None, :, None])}
    for l in range(LMAX + 1):
        words, scales = pack_weight(np.random.standard_normal((MI, MO)) / np.sqrt(MI) / s[:, None], FMT)
        d["w%d_words" % l] = words
        d["w%d_scales" % l] = scales
    return d


def reference(x, w0_words, w0_scales, w1_words, w1_scales, w2_words, w2_scales, w3_words, w3_scales):
    xq = mxq(f64(x), 1, "e4m3")
    parts = []
    packed = [(w0_words, w0_scales), (w1_words, w1_scales), (w2_words, w2_scales), (w3_words, w3_scales)]
    for l, (words, scales) in enumerate(packed):
        xl = xq[:, :, l * l:(l + 1) ** 2].transpose(0, 2, 1)
        parts.append((xl @ unpack_weight(words, scales, FMT)).transpose(0, 2, 1))
    return np.concatenate(parts, axis=2)

@@ -1,0 +1,162 @@
+from contextlib import ExitStack
+
+import concourse.bass as bass
+import concourse.mybir as mybir
+import concourse.tile as tile
+from concourse.masks import make_identity
+
+F32 = mybir.dt.float32
+BF16 = mybir.dt.bfloat16
+I32 = mybir.dt.int32
+U32 = mybir.dt.uint32
+U8 = mybir.dt.uint8
+FP8X4 = mybir.dt.float8_e4m3fn_x4
+ADD = mybir.AluOpType.add
+
+P = 128
+NB = 16
+CH = 16
+G = 4
+HALF = 1024
+FLOPS = 2 * NB * CH * 2048 * 2048
+
+WINDOW = {0: 0, 1: 0, 2: 64, 3: 128}
+QUADS_DONE = {3: (3,), 2: (2, 1), 1: (), 0: (0,)}
+
+
+def tile_irrepsstridelinear_w_kernel(
+    tc, x, w0_words, w0_scales, w1_words, w1_scales, w2_words, w2_scales, w3_words, w3_scales, out
+):
+    nc = tc.nc
+    words = (w0_words, w1_words, w2_words, w3_words)
+    scales = (w0_scales, w1_scales, w2_scales, w3_scales)
+    degrees = (3, 2, 1, 0)
+    stages = [(h, l) for h in range(2) for l in degrees]
+
+    with ExitStack() as ctx:
+        keep = ctx.enter_context(tc.tile_pool(name="keep", bufs=1))
+        psum_acc = ctx.enter_context(tc.psum_pool(name="acc", bufs=4))
+        psum_tr = ctx.enter_context(tc.psum_pool(name="tr", bufs=4))
+        ctx.enter_context(tc.manual_schedule())
+
+        raw = keep.tile([P, NB, G, 64], BF16)
+        nc.scalar.dma_start(out=raw[:], in_=x.rearrange("n (g p t) c -> p n g (t c)", g=G, p=P, t=4))
+
+        planes = keep.tile([P, 4, 2048], U8, align_bytes=64)
+        for l in degrees:
+            nc.vector.memset(planes[:, l, :].bitcast(I32), 0)
+        for l in degrees:
+            for q in range(4):
+                nc.sync.dma_start(
+                    out=planes[32 * q : 32 * q + 16, l, :].bitcast(I32),
+                    in_=scales[l][:, 4 * q : 4 * q + 4, :].bitcast(I32),
+                )
+
+        ident = keep.tile([P, P], F32)
+        make_identity(nc, ident[:])
+
+        wt = {}
+        for h, l in stages:
+            for g in range(G):
+                w_tile = keep.tile([P, HALF], U32, name="w%d_%d_%d" % (l, h, g), align_bytes=64)
+                nc.sync.dma_start(
+                    out=w_tile[:].bitcast(I32),
+                    in_=words[l][g].rearrange("p n t -> p (n t)")[:, 4 * HALF * h : 4 * HALF * (h + 1)].bitcast(I32),
+                )
+                wt[(h, l, g)] = w_tile
+
+        grouped = keep.tile([P, G, CH, NB, 4], BF16, align_bytes=64)
+        x_codes = keep.tile([P, G, CH * NB], U32, align_bytes=64)
+        x_scales = keep.tile([P, G, CH * NB], U8, align_bytes=64)
+        for g in range(G):
+            src = raw[:, :, g, :].rearrange("p n (t c) -> p c n t", t=4, c=CH)
+            if g % 2 == 0:
+                nc.vector.tensor_copy(out=grouped[:, g], in_=src)
+            else:
+                nc.scalar.copy(out=grouped[:, g], in_=src)
+        for g in range(G):
+            nc.vector.quantize_mx(
+                out=x_codes[:, g, :].bitcast(FP8X4),
+                scales=x_scales[:, g, :],
+                in_=grouped[:, g].rearrange("p c n t -> p (c n t)"),
+            )
+
+        res = keep.tile([P, 2, CH, NB, 8], F32)
+        fin = keep.tile([P, 2, P, CH], F32)
+        out_view = out.rearrange("n (h a b) c -> h n a (b c)", h=2, a=8, b=P)
+        tr_tiles = {}
+
+        def mx_pass(acc, j, h, l, a, g, start, stop):
+            w0 = WINDOW[l]
+            nc.tensor.matmul_mx(
+                out=acc[:, j, :],
+                lhsT=wt[(h, l, g)][:, P * a : P * (a + 1)].bitcast(FP8X4),
+                lhsT_scale=planes[4 * g : P, l, HALF * h + P * a : HALF * h + P * (a + 1)],
+                rhs=x_codes[:, g, w0 : w0 + P].bitcast(FP8X4),
+                rhs_scale=x_scales[:, g, w0 : w0 + P],
+                start=start,
+                stop=stop,
+            )
+
+        def views(acc, h, l, b):
+            c0 = l * l
+            c1 = (l + 1) * (l + 1)
+            w0 = WINDOW[l]
+            src = acc[:, :, NB * c0 - w0 : NB * c1 - w0].rearrange("p j (c n) -> p c n j", n=NB)
+            dst = res[:, h, c0:c1, :, 4 * b : 4 * b + 4]
+            return src, dst
+
+        def passes(h, l):
+            for b in range(2):
+                acc = psum_acc.tile([P, 4, P], F32, name="acc")
+                for j in range(4):
+                    for g in range(G):
+                        mx_pass(acc, j, h, l, 4 * b + j, g, g == 0, g == G - 1)
+                src, dst = views(acc, h, l, b)
+                if l in (3, 0):
+                    nc.vector.tensor_copy(out=dst, in_=src)
+                else:
+                    nc.scalar.copy(out=dst, in_=src)
+
+        def lone_passes(h, l, g):
+            for b in range(2):
+                acc = psum_acc.tile([P, 4, P], F32, name="acc")
+                for j in range(4):
+                    mx_pass(acc, j, h, l, 4 * b + j, g, True, True)
+                src, dst = views(acc, h, l, b)
+                if g == 0:
+                    nc.vector.tensor_copy(out=dst, in_=src)
+                else:
+                    nc.vector.tensor_tensor(out=dst, in0=src, in1=dst, op=ADD)
+
+        def finish(h, l):
+            for c in range(l * l, (l + 1) * (l + 1)):
+                q = c // 4
+                if (h, q) not in tr_tiles:
+                    tr_tiles[(h, q)] = psum_tr.tile([P, 4, P], F32, name="tr")
+                nc.tensor.transpose(
+                    out=tr_tiles[(h, q)][:, c % 4, :],
+                    in_=res[:, h, c].rearrange("p n a -> p (n a)"),
+                    identity=ident[:],
+                )
+            for q in QUADS_DONE[l]:
+                src = tr_tiles[(h, q)][:].rearrange("p q o -> p o q")
+                dst = fin[:, h, :, 4 * q : 4 * q + 4]
+                if q >= 2:
+                    nc.vector.tensor_copy(out=dst, in_=src)
+                else:
+                    nc.scalar.copy(out=dst, in_=src)
+            if l == 0:
+                nc.sync.dma_start(out=out_view[h], in_=fin[:, h].rearrange("p o c -> p (o c)"))
+
+        before = None
+        for h, l in stages[:-1]:
+            passes(h, l)
+            if before is not None:
+                finish(before[0], before[1])
+            before = (h, l)
+        for g in range(G - 1):
+            lone_passes(1, 0, g)
+        finish(before[0], before[1])
+        lone_passes(1, 0, G - 1)
+        finish(1, 0)

@@ -39,8 +39,8 @@ def tile_irrepsstridelinear_w_kernel(
         psum_tr = ctx.enter_context(tc.psum_pool(name="tr", bufs=4))
         ctx.enter_context(tc.manual_schedule())
 
-        raw = keep.tile([P, NB, G, 64], BF16)
-        nc.scalar.dma_start(out=raw[:], in_=x.rearrange("n (g p t) c -> p n g (t c)", g=G, p=P, t=4))
+        rows = keep.tile([P, 8192], BF16)
+        nc.scalar.dma_start(out=rows[32:96, :], in_=x.rearrange("n (g q) c -> (n g) (q c)", g=G))
 
         planes = keep.tile([P, 4, 2048], U8, align_bytes=64)
         for l in degrees:
@@ -54,6 +54,8 @@ def tile_irrepsstridelinear_w_kernel(
 
         ident = keep.tile([P, P], F32)
         make_identity(nc, ident[:])
+        nc.vector.memset(rows[0:32, :].bitcast(I32), 0)
+        nc.gpsimd.memset(rows[96:128, :].bitcast(F32), 0.0)
 
         wt = {}
         for h, l in stages:
@@ -68,12 +70,21 @@ def tile_irrepsstridelinear_w_kernel(
         grouped = keep.tile([P, G, CH, NB, 4], BF16, align_bytes=64)
         x_codes = keep.tile([P, G, CH * NB], U32, align_bytes=64)
         x_scales = keep.tile([P, G, CH * NB], U8, align_bytes=64)
-        for g in range(G):
-            src = raw[:, :, g, :].rearrange("p n (t c) -> p c n t", t=4, c=CH)
-            if g % 2 == 0:
-                nc.vector.tensor_copy(out=grouped[:, g], in_=src)
+        row_words = rows[:].bitcast(F32)
+        for d in range(CH // 2):
+            if d % 2 == 0:
+                bank = psum_acc.tile([P, 4, P], F32, name="acc")
             else:
-                nc.scalar.copy(out=grouped[:, g], in_=src)
+                bank = psum_tr.tile([P, 4, P], F32, name="tr")
+            for t in range(4):
+                nc.tensor.transpose(out=bank[:, t, :], in_=row_words[:, 8 * t + d : 4096 : 32], identity=ident[:])
+            halves = bank[:].bitcast(BF16).rearrange("p t (s e) -> p t s e", e=2)
+            for e in range(2):
+                src = halves[:, :, 32:96, e].rearrange("p t (n g) -> p g n t", g=G)
+                if d % 2 == 0:
+                    nc.vector.tensor_copy(out=grouped[:, :, 2 * d + e, :, :], in_=src)
+                else:
+                    nc.scalar.copy(out=grouped[:, :, 2 * d + e, :, :], in_=src)
         for g in range(G):
             nc.vector.quantize_mx(
                 out=x_codes[:, g, :].bitcast(FP8X4),

@@ -43,19 +43,25 @@ def tile_irrepsstridelinear_w_kernel(
         nc.scalar.dma_start(out=rows[32:96, :], in_=x.rearrange("n (g q) c -> (n g) (q c)", g=G))
 
         planes = keep.tile([P, 4, 2048], U8, align_bytes=64)
-        for l in degrees:
-            nc.vector.memset(planes[:, l, :].bitcast(I32), 0)
-        for l in degrees:
-            for q in range(4):
-                nc.sync.dma_start(
-                    out=planes[32 * q : 32 * q + 16, l, :].bitcast(I32),
-                    in_=scales[l][:, 4 * q : 4 * q + 4, :].bitcast(I32),
-                )
-
-        ident = keep.tile([P, P], F32)
-        make_identity(nc, ident[:])
+        nc.vector.memset(planes[:, 3, :].bitcast(I32), 0)
         nc.vector.memset(rows[0:32, :].bitcast(I32), 0)
         nc.gpsimd.memset(rows[96:128, :].bitcast(F32), 0.0)
+        for l in (2, 1, 0):
+            nc.vector.memset(planes[:, l, :].bitcast(I32), 0)
+        ident = keep.tile([P, P], F32)
+        make_identity(nc, ident[:])
+        for l in degrees:
+            for q in range(4):
+                if l == 3:
+                    nc.sync.dma_start(
+                        out=planes[32 * q : 32 * q + 16, l, :].bitcast(I32),
+                        in_=scales[l][:, 4 * q : 4 * q + 4, :].bitcast(I32),
+                    )
+                else:
+                    nc.gpsimd.dma_start(
+                        out=planes[32 * q : 32 * q + 16, l, :].bitcast(F32),
+                        in_=scales[l][:, 4 * q : 4 * q + 4, :].bitcast(F32),
+                    )
 
         wt = {}
         for h, l in stages:
@@ -71,17 +77,21 @@ def tile_irrepsstridelinear_w_kernel(
         x_codes = keep.tile([P, G, CH * NB], U32, align_bytes=64)
         x_scales = keep.tile([P, G, CH * NB], U8, align_bytes=64)
         row_words = rows[:].bitcast(F32)
+        sorted_words = keep.tile([P, 32, P], F32)
+        by_plane = row_words.rearrange("s (p t d) -> s d t p", t=4, d=8)
+        for d in range(CH // 2):
+            nc.vector.tensor_copy(out=sorted_words[:, 4 * d : 4 * d + 4, :], in_=by_plane[:, d])
         for d in range(CH // 2):
             if d % 2 == 0:
                 bank = psum_acc.tile([P, 4, P], F32, name="acc")
             else:
                 bank = psum_tr.tile([P, 4, P], F32, name="tr")
             for t in range(4):
-                nc.tensor.transpose(out=bank[:, t, :], in_=row_words[:, 8 * t + d : 4096 : 32], identity=ident[:])
+                nc.tensor.transpose(out=bank[:, t, :], in_=sorted_words[:, 4 * d + t, :], identity=ident[:])
             halves = bank[:].bitcast(BF16).rearrange("p t (s e) -> p t s e", e=2)
             for e in range(2):
                 src = halves[:, :, 32:96, e].rearrange("p t (n g) -> p g n t", g=G)
-                if d % 2 == 0:
+                if d >= 6:
                     nc.vector.tensor_copy(out=grouped[:, :, 2 * d + e, :, :], in_=src)
                 else:
                     nc.scalar.copy(out=grouped[:, :, 2 * d + e, :, :], in_=src)

@@ -1,8 +1,6 @@
 from contextlib import ExitStack
 
-import concourse.bass as bass
 import concourse.mybir as mybir
-import concourse.tile as tile
 from concourse.masks import make_identity
 
 F32 = mybir.dt.float32
@@ -11,17 +9,17 @@ I32 = mybir.dt.int32
 U32 = mybir.dt.uint32
 U8 = mybir.dt.uint8
 FP8X4 = mybir.dt.float8_e4m3fn_x4
-ADD = mybir.AluOpType.add
 
 P = 128
 NB = 16
 CH = 16
 G = 4
-HALF = 1024
 FLOPS = 2 * NB * CH * 2048 * 2048
 
-WINDOW = {0: 0, 1: 0, 2: 64, 3: 128}
-QUADS_DONE = {3: (3,), 2: (2, 1), 1: (), 0: (0,)}
+WINDOW = {1: 0, 2: 64, 3: 128}
+QUADS_DONE = {3: (3,), 2: (2, 1), 1: (0,)}
+PIECES = {3: ((0, 2048),), 2: ((0, 2048),), 1: ((0, 1024), (1024, 1024)), 0: ((0, 1024), (1024, 512), (1536, 512))}
+DIAG = 516
 
 
 def tile_irrepsstridelinear_w_kernel(
@@ -31,7 +29,6 @@ def tile_irrepsstridelinear_w_kernel(
     words = (w0_words, w1_words, w2_words, w3_words)
     scales = (w0_scales, w1_scales, w2_scales, w3_scales)
     degrees = (3, 2, 1, 0)
-    stages = [(h, l) for h in range(2) for l in degrees]
 
     with ExitStack() as ctx:
         keep = ctx.enter_context(tc.tile_pool(name="keep", bufs=1))
@@ -39,59 +36,53 @@ def tile_irrepsstridelinear_w_kernel(
         psum_tr = ctx.enter_context(tc.psum_pool(name="tr", bufs=4))
         ctx.enter_context(tc.manual_schedule())
 
-        rows = keep.tile([P, 8192], BF16)
+        rows = keep.tile([P, 8192], BF16, name="rows", tag="rows_then_masks", align_bytes=64)
         nc.scalar.dma_start(out=rows[32:96, :], in_=x.rearrange("n (g q) c -> (n g) (q c)", g=G))
 
         planes = keep.tile([P, 4, 2048], U8, align_bytes=64)
-        nc.vector.memset(planes[:, 3, :].bitcast(I32), 0)
-        nc.vector.memset(rows[0:32, :].bitcast(I32), 0)
-        nc.gpsimd.memset(rows[96:128, :].bitcast(F32), 0.0)
-        for l in (2, 1, 0):
+        for l in degrees:
             nc.vector.memset(planes[:, l, :].bitcast(I32), 0)
-        ident = keep.tile([P, P], F32)
-        make_identity(nc, ident[:])
         for l in degrees:
             for q in range(4):
-                if l == 3:
-                    nc.sync.dma_start(
-                        out=planes[32 * q : 32 * q + 16, l, :].bitcast(I32),
-                        in_=scales[l][:, 4 * q : 4 * q + 4, :].bitcast(I32),
-                    )
-                else:
-                    nc.gpsimd.dma_start(
-                        out=planes[32 * q : 32 * q + 16, l, :].bitcast(F32),
-                        in_=scales[l][:, 4 * q : 4 * q + 4, :].bitcast(F32),
-                    )
+                nc.sync.dma_start(
+                    out=planes[32 * q : 32 * q + 16, l, :].bitcast(I32),
+                    in_=scales[l][:, 4 * q : 4 * q + 4, :].bitcast(I32),
+                )
+
+        ident = keep.tile([P, P], F32)
+        make_identity(nc, ident[:])
+        nc.vector.memset(rows[0:32, :].bitcast(I32), 0)
+        nc.gpsimd.memset(rows[96:128, :].bitcast(F32), 0.0)
+        diag = keep.tile([P, 8 * DIAG], BF16, align_bytes=64)
+        nc.vector.memset(diag[:].bitcast(I32), 0)
 
         wt = {}
-        for h, l in stages:
-            for g in range(G):
-                w_tile = keep.tile([P, HALF], U32, name="w%d_%d_%d" % (l, h, g), align_bytes=64)
-                nc.sync.dma_start(
-                    out=w_tile[:].bitcast(I32),
-                    in_=words[l][g].rearrange("p n t -> p (n t)")[:, 4 * HALF * h : 4 * HALF * (h + 1)].bitcast(I32),
-                )
-                wt[(h, l, g)] = w_tile
+        for l in degrees:
+            for first, width in PIECES[l]:
+                for g in range(G):
+                    w_tile = keep.tile([P, width], U32, name="w%d_%d_%d" % (l, first, g), align_bytes=64)
+                    nc.sync.dma_start(
+                        out=w_tile[:].bitcast(I32),
+                        in_=words[l][g].rearrange("p n t -> p (n t)")[:, 4 * first : 4 * (first + width)].bitcast(I32),
+                    )
+                    for ot in range(first // P, (first + width) // P):
+                        wt[(l, g, ot)] = w_tile[:, P * ot - first : P * (ot + 1) - first]
 
         grouped = keep.tile([P, G, CH, NB, 4], BF16, align_bytes=64)
         x_codes = keep.tile([P, G, CH * NB], U32, align_bytes=64)
         x_scales = keep.tile([P, G, CH * NB], U8, align_bytes=64)
         row_words = rows[:].bitcast(F32)
-        sorted_words = keep.tile([P, 32, P], F32)
-        by_plane = row_words.rearrange("s (p t d) -> s d t p", t=4, d=8)
-        for d in range(CH // 2):
-            nc.vector.tensor_copy(out=sorted_words[:, 4 * d : 4 * d + 4, :], in_=by_plane[:, d])
         for d in range(CH // 2):
             if d % 2 == 0:
                 bank = psum_acc.tile([P, 4, P], F32, name="acc")
             else:
                 bank = psum_tr.tile([P, 4, P], F32, name="tr")
             for t in range(4):
-                nc.tensor.transpose(out=bank[:, t, :], in_=sorted_words[:, 4 * d + t, :], identity=ident[:])
+                nc.tensor.transpose(out=bank[:, t, :], in_=row_words[:, 8 * t + d : 4096 : 32], identity=ident[:])
             halves = bank[:].bitcast(BF16).rearrange("p t (s e) -> p t s e", e=2)
             for e in range(2):
                 src = halves[:, :, 32:96, e].rearrange("p t (n g) -> p g n t", g=G)
-                if d >= 6:
+                if d % 2 == 0:
                     nc.vector.tensor_copy(out=grouped[:, :, 2 * d + e, :, :], in_=src)
                 else:
                     nc.scalar.copy(out=grouped[:, :, 2 * d + e, :, :], in_=src)
@@ -103,81 +94,113 @@ def tile_irrepsstridelinear_w_kernel(
             )
 
         res = keep.tile([P, 2, CH, NB, 8], F32)
-        fin = keep.tile([P, 2, P, CH], F32)
-        out_view = out.rearrange("n (h a b) c -> h n a (b c)", h=2, a=8, b=P)
+        fins = [keep.tile([P, P, CH], F32, name="fin%d" % i) for i in range(3)]
+        mask_codes = keep.tile([P, G, 8, P], U32, name="mask_codes", tag="rows_then_masks", align_bytes=64)
+        mask_scales = keep.tile([P, G, 8, P], U8, align_bytes=64)
         tr_tiles = {}
 
-        def mx_pass(acc, j, h, l, a, g, start, stop):
-            w0 = WINDOW[l]
-            nc.tensor.matmul_mx(
-                out=acc[:, j, :],
-                lhsT=wt[(h, l, g)][:, P * a : P * (a + 1)].bitcast(FP8X4),
-                lhsT_scale=planes[4 * g : P, l, HALF * h + P * a : HALF * h + P * (a + 1)],
-                rhs=x_codes[:, g, w0 : w0 + P].bitcast(FP8X4),
-                rhs_scale=x_scales[:, g, w0 : w0 + P],
-                start=start,
-                stop=stop,
-            )
+        def tile_of(block, a):
+            if block == 0:
+                return a
+            return 8 + 4 * (a % 2) + a // 2
 
-        def views(acc, h, l, b):
+        def build_masks():
+            spots = diag[:].rearrange("p (a r) -> p a r", r=DIAG)[:, :, 0:512]
+            spots = spots.rearrange("p a (n s) -> p a n s", s=32)[:, :, :, 0:4]
+            for g in range(G):
+                nc.vector.tensor_copy(
+                    out=spots, in_=grouped[:, g, 0, :, :].unsqueeze(1).to_broadcast([P, 8, NB, 4])
+                )
+                nc.vector.quantize_mx(
+                    out=mask_codes[:, g].rearrange("p a j -> p (a j)").bitcast(FP8X4),
+                    scales=mask_scales[:, g].rearrange("p a j -> p (a j)"),
+                    in_=diag[:, 0:4096],
+                )
+
+        def passes(l, block):
             c0 = l * l
             c1 = (l + 1) * (l + 1)
             w0 = WINDOW[l]
-            src = acc[:, :, NB * c0 - w0 : NB * c1 - w0].rearrange("p j (c n) -> p c n j", n=NB)
-            dst = res[:, h, c0:c1, :, 4 * b : 4 * b + 4]
-            return src, dst
-
-        def passes(h, l):
             for b in range(2):
                 acc = psum_acc.tile([P, 4, P], F32, name="acc")
                 for j in range(4):
+                    ot = tile_of(block, 4 * b + j)
                     for g in range(G):
-                        mx_pass(acc, j, h, l, 4 * b + j, g, g == 0, g == G - 1)
-                src, dst = views(acc, h, l, b)
-                if l in (3, 0):
+                        nc.tensor.matmul_mx(
+                            out=acc[:, j, :],
+                            lhsT=wt[(l, g, ot)].bitcast(FP8X4),
+                            lhsT_scale=planes[4 * g : P, l, P * ot : P * (ot + 1)],
+                            rhs=x_codes[:, g, w0 : w0 + P].bitcast(FP8X4),
+                            rhs_scale=x_scales[:, g, w0 : w0 + P],
+                            start=(g == 0),
+                            stop=(g == G - 1),
+                        )
+                src = acc[:, :, NB * c0 - w0 : NB * c1 - w0].rearrange("p j (c n) -> p c n j", n=NB)
+                dst = res[:, block, c0:c1, :, 4 * b : 4 * b + 4]
+                if l == 3:
                     nc.vector.tensor_copy(out=dst, in_=src)
                 else:
                     nc.scalar.copy(out=dst, in_=src)
 
-        def lone_passes(h, l, g):
-            for b in range(2):
-                acc = psum_acc.tile([P, 4, P], F32, name="acc")
-                for j in range(4):
-                    mx_pass(acc, j, h, l, 4 * b + j, g, True, True)
-                src, dst = views(acc, h, l, b)
-                if g == 0:
-                    nc.vector.tensor_copy(out=dst, in_=src)
-                else:
-                    nc.vector.tensor_tensor(out=dst, in0=src, in1=dst, op=ADD)
-
-        def finish(h, l):
+        def finish(l, block):
             for c in range(l * l, (l + 1) * (l + 1)):
                 q = c // 4
-                if (h, q) not in tr_tiles:
-                    tr_tiles[(h, q)] = psum_tr.tile([P, 4, P], F32, name="tr")
+                if (block, q) not in tr_tiles:
+                    tr_tiles[(block, q)] = psum_tr.tile([P, 4, P], F32, name="tr")
                 nc.tensor.transpose(
-                    out=tr_tiles[(h, q)][:, c % 4, :],
-                    in_=res[:, h, c].rearrange("p n a -> p (n a)"),
+                    out=tr_tiles[(block, q)][:, c % 4, :],
+                    in_=res[:, block, c].rearrange("p n a -> p (n a)"),
                     identity=ident[:],
                 )
             for q in QUADS_DONE[l]:
-                src = tr_tiles[(h, q)][:].rearrange("p q o -> p o q")
-                dst = fin[:, h, :, 4 * q : 4 * q + 4]
-                if q >= 2:
-                    nc.vector.tensor_copy(out=dst, in_=src)
-                else:
-                    nc.scalar.copy(out=dst, in_=src)
-            if l == 0:
-                nc.sync.dma_start(out=out_view[h], in_=fin[:, h].rearrange("p o c -> p (o c)"))
+                lo = 1 if q == 0 else 0
+                src = tr_tiles[(block, q)][:, lo:4, :].rearrange("p q o -> p o q")
+                for fin in fins[0:1] if block == 0 else fins[1:3]:
+                    dst = fin[:, :, 4 * q + lo : 4 * q + 4]
+                    if q >= 2:
+                        nc.vector.tensor_copy(out=dst, in_=src)
+                    else:
+                        nc.scalar.copy(out=dst, in_=src)
 
-        before = None
-        for h, l in stages[:-1]:
-            passes(h, l)
-            if before is not None:
-                finish(before[0], before[1])
-            before = (h, l)
-        for g in range(G - 1):
-            lone_passes(1, 0, g)
-        finish(before[0], before[1])
-        lone_passes(1, 0, G - 1)
+        def direct(i, between):
+            block = 0 if i == 0 else 1
+            places = list(range(8)) if i == 0 else list(range(i - 1, 8, 2))
+            acc = psum_acc.tile([P, 4, P], F32, name="acc")
+            for g in range(G):
+                for a in places:
+                    ot = tile_of(block, a)
+                    nc.tensor.matmul_mx(
+                        out=acc[:, 0, :],
+                        lhsT=mask_codes[:, g, a, :].bitcast(FP8X4),
+                        lhsT_scale=mask_scales[:, g, a, :],
+                        rhs=wt[(0, g, ot)].bitcast(FP8X4),
+                        rhs_scale=planes[4 * g : P, 0, P * ot : P * (ot + 1)],
+                        start=(g == 0 and a == places[0]),
+                        stop=(g == G - 1 and a == places[-1]),
+                    )
+                if g == 0 and between:
+                    finish(1, 1)
+            nc.scalar.copy(out=fins[i][:, :, 0], in_=acc[:, 0, :])
+            flat = fins[i][:].rearrange("p o c -> p (o c)")
+            if i == 0:
+                nc.sync.dma_start(out=out.rearrange("n (h a b) c -> h n a (b c)", h=2, a=8, b=P)[0], in_=flat)
+            else:
+                nc.sync.dma_start(
+                    out=out.rearrange("n (r a b) c -> r n a (b c)", r=4, a=4, b=P)[i + 1], in_=flat[i - 1 : P : 2, :]
+                )
+
+        passes(3, 0)
+        passes(3, 1)
+        build_masks()
+        passes(2, 0)
+        passes(2, 1)
+        finish(3, 0)
+        finish(3, 1)
+        passes(1, 0)
+        finish(2, 0)
+        finish(2, 1)
+        passes(1, 1)
         finish(1, 0)
+        direct(0, True)
+        direct(1, False)
+        direct(2, False)

@@ -42,17 +42,22 @@ def tile_irrepsstridelinear_w_kernel(
         planes = keep.tile([P, 4, 2048], U8, align_bytes=64)
         for l in degrees:
             nc.vector.memset(planes[:, l, :].bitcast(I32), 0)
-        for l in degrees:
-            for q in range(4):
-                nc.sync.dma_start(
-                    out=planes[32 * q : 32 * q + 16, l, :].bitcast(I32),
-                    in_=scales[l][:, 4 * q : 4 * q + 4, :].bitcast(I32),
-                )
+        for q in range(4):
+            nc.sync.dma_start(
+                out=planes[32 * q : 32 * q + 16, 3, :].bitcast(I32),
+                in_=scales[3][:, 4 * q : 4 * q + 4, :].bitcast(I32),
+            )
 
         ident = keep.tile([P, P], F32)
         make_identity(nc, ident[:])
         nc.vector.memset(rows[0:32, :].bitcast(I32), 0)
         nc.gpsimd.memset(rows[96:128, :].bitcast(F32), 0.0)
+        for l in (2, 1, 0):
+            for q in range(4):
+                nc.gpsimd.dma_start(
+                    out=planes[32 * q : 32 * q + 16, l, :].bitcast(F32),
+                    in_=scales[l][:, 4 * q : 4 * q + 4, :].bitcast(F32),
+                )
         diag = keep.tile([P, 8 * DIAG], BF16, align_bytes=64)
         nc.vector.memset(diag[:].bitcast(I32), 0)
 

@@ -37,15 +37,15 @@ def tile_irrepsstridelinear_w_kernel(
         ctx.enter_context(tc.manual_schedule())
 
         rows = keep.tile([P, 8192], BF16, name="rows", tag="rows_then_masks", align_bytes=64)
-        nc.scalar.dma_start(out=rows[32:96, :], in_=x.rearrange("n (g q) c -> (n g) (q c)", g=G))
+        nc.sync.dma_start(out=rows[32:96, :], in_=x.rearrange("n (g q) c -> (n g) (q c)", g=G))
 
         planes = keep.tile([P, 4, 2048], U8, align_bytes=64)
         for l in degrees:
             nc.vector.memset(planes[:, l, :].bitcast(I32), 0)
         for q in range(4):
-            nc.sync.dma_start(
-                out=planes[32 * q : 32 * q + 16, 3, :].bitcast(I32),
-                in_=scales[3][:, 4 * q : 4 * q + 4, :].bitcast(I32),
+            nc.scalar.dma_start(
+                out=planes[32 * q : 32 * q + 16, 3, :].bitcast(F32),
+                in_=scales[3][:, 4 * q : 4 * q + 4, :].bitcast(F32),
             )
 
         ident = keep.tile([P, P], F32)
@@ -196,13 +196,13 @@ def tile_irrepsstridelinear_w_kernel(
 
         passes(3, 0)
         passes(3, 1)
+        finish(3, 0)
+        finish(3, 1)
         build_masks()
         passes(2, 0)
         passes(2, 1)
-        finish(3, 0)
-        finish(3, 1)
-        passes(1, 0)
         finish(2, 0)
+        passes(1, 0)
         finish(2, 1)
         passes(1, 1)
         finish(1, 0)

@@ -17,8 +17,9 @@ G = 4
 FLOPS = 2 * NB * CH * 2048 * 2048
 
 WINDOW = {1: 0, 2: 64, 3: 128}
-QUADS_DONE = {3: (3,), 2: (2, 1), 1: (0,)}
 PIECES = {3: ((0, 2048),), 2: ((0, 2048),), 1: ((0, 1024), (1024, 1024)), 0: ((0, 1024), (1024, 512), (1536, 512))}
+Q = 4
+EDGE = 32
 DIAG = 516
 
 
@@ -58,7 +59,7 @@ def tile_irrepsstridelinear_w_kernel(
                     out=planes[32 * q : 32 * q + 16, l, :].bitcast(F32),
                     in_=scales[l][:, 4 * q : 4 * q + 4, :].bitcast(F32),
                 )
-        diag = keep.tile([P, 8 * DIAG], BF16, align_bytes=64)
+        diag = keep.tile([P, 4 * DIAG], BF16, align_bytes=64)
         nc.vector.memset(diag[:].bitcast(I32), 0)
 
         wt = {}
@@ -98,114 +99,123 @@ def tile_irrepsstridelinear_w_kernel(
                 in_=grouped[:, g].rearrange("p c n t -> p (c n t)"),
             )
 
-        res = keep.tile([P, 2, CH, NB, 8], F32)
-        fins = [keep.tile([P, P, CH], F32, name="fin%d" % i) for i in range(3)]
-        mask_codes = keep.tile([P, G, 8, P], U32, name="mask_codes", tag="rows_then_masks", align_bytes=64)
-        mask_scales = keep.tile([P, G, 8, P], U8, align_bytes=64)
-        tr_tiles = {}
-
-        def tile_of(block, a):
-            if block == 0:
-                return a
-            return 8 + 4 * (a % 2) + a // 2
+        res = {}
+        for l in (3, 2, 1):
+            res[l] = keep.tile([P, Q + 1, EDGE + 64 * (2 * l + 1)], F32, name="res%d" % l)
+            nc.vector.memset(res[l][:, :, 0:EDGE], 0.0)
+        fins = [keep.tile([P, P, CH], F32, name="fin%d" % i) for i in range(Q)]
+        mask_codes = keep.tile([P, G, 4, P], U32, name="mask_codes", tag="rows_then_masks", align_bytes=64)
+        mask_scales = keep.tile([P, G, 4, P], U8, align_bytes=64)
 
         def build_masks():
-            spots = diag[:].rearrange("p (a r) -> p a r", r=DIAG)[:, :, 0:512]
-            spots = spots.rearrange("p a (n s) -> p a n s", s=32)[:, :, :, 0:4]
+            spots = diag[:].rearrange("p (a r) -> p a r", r=DIAG)[:, :, 4 * EDGE : 4 * EDGE + 256]
+            spots = spots.rearrange("p a (n s) -> p a n s", s=16)[:, :, :, 0:4]
             for g in range(G):
                 nc.vector.tensor_copy(
-                    out=spots, in_=grouped[:, g, 0, :, :].unsqueeze(1).to_broadcast([P, 8, NB, 4])
+                    out=spots, in_=grouped[:, g, 0, :, :].unsqueeze(1).to_broadcast([P, 4, NB, 4])
                 )
                 nc.vector.quantize_mx(
                     out=mask_codes[:, g].rearrange("p a j -> p (a j)").bitcast(FP8X4),
                     scales=mask_scales[:, g].rearrange("p a j -> p (a j)"),
-                    in_=diag[:, 0:4096],
+                    in_=diag[:, 0:2048],
                 )
 
-        def passes(l, block):
+        def passes(l, q):
             c0 = l * l
             c1 = (l + 1) * (l + 1)
             w0 = WINDOW[l]
-            for b in range(2):
-                acc = psum_acc.tile([P, 4, P], F32, name="acc")
-                for j in range(4):
-                    ot = tile_of(block, 4 * b + j)
-                    for g in range(G):
-                        nc.tensor.matmul_mx(
-                            out=acc[:, j, :],
-                            lhsT=wt[(l, g, ot)].bitcast(FP8X4),
-                            lhsT_scale=planes[4 * g : P, l, P * ot : P * (ot + 1)],
-                            rhs=x_codes[:, g, w0 : w0 + P].bitcast(FP8X4),
-                            rhs_scale=x_scales[:, g, w0 : w0 + P],
-                            start=(g == 0),
-                            stop=(g == G - 1),
-                        )
-                src = acc[:, :, NB * c0 - w0 : NB * c1 - w0].rearrange("p j (c n) -> p c n j", n=NB)
-                dst = res[:, block, c0:c1, :, 4 * b : 4 * b + 4]
-                if l == 3:
-                    nc.vector.tensor_copy(out=dst, in_=src)
-                else:
-                    nc.scalar.copy(out=dst, in_=src)
-
-        def finish(l, block):
-            for c in range(l * l, (l + 1) * (l + 1)):
-                q = c // 4
-                if (block, q) not in tr_tiles:
-                    tr_tiles[(block, q)] = psum_tr.tile([P, 4, P], F32, name="tr")
-                nc.tensor.transpose(
-                    out=tr_tiles[(block, q)][:, c % 4, :],
-                    in_=res[:, block, c].rearrange("p n a -> p (n a)"),
-                    identity=ident[:],
-                )
-            for q in QUADS_DONE[l]:
-                lo = 1 if q == 0 else 0
-                src = tr_tiles[(block, q)][:, lo:4, :].rearrange("p q o -> p o q")
-                for fin in fins[0:1] if block == 0 else fins[1:3]:
-                    dst = fin[:, :, 4 * q + lo : 4 * q + 4]
-                    if q >= 2:
-                        nc.vector.tensor_copy(out=dst, in_=src)
-                    else:
-                        nc.scalar.copy(out=dst, in_=src)
-
-        def direct(i, between):
-            block = 0 if i == 0 else 1
-            places = list(range(8)) if i == 0 else list(range(i - 1, 8, 2))
             acc = psum_acc.tile([P, 4, P], F32, name="acc")
-            for g in range(G):
-                for a in places:
-                    ot = tile_of(block, a)
+            for j in range(4):
+                ot = 4 * q + j
+                for g in range(G):
                     nc.tensor.matmul_mx(
-                        out=acc[:, 0, :],
-                        lhsT=mask_codes[:, g, a, :].bitcast(FP8X4),
-                        lhsT_scale=mask_scales[:, g, a, :],
-                        rhs=wt[(0, g, ot)].bitcast(FP8X4),
-                        rhs_scale=planes[4 * g : P, 0, P * ot : P * (ot + 1)],
-                        start=(g == 0 and a == places[0]),
-                        stop=(g == G - 1 and a == places[-1]),
+                        out=acc[:, j, :],
+                        lhsT=wt[(l, g, ot)].bitcast(FP8X4),
+                        lhsT_scale=planes[4 * g : P, l, P * ot : P * (ot + 1)],
+                        rhs=x_codes[:, g, w0 : w0 + P].bitcast(FP8X4),
+                        rhs_scale=x_scales[:, g, w0 : w0 + P],
+                        start=(g == 0),
+                        stop=(g == G - 1),
                     )
-                if g == 0 and between:
-                    finish(1, 1)
-            nc.scalar.copy(out=fins[i][:, :, 0], in_=acc[:, 0, :])
-            flat = fins[i][:].rearrange("p o c -> p (o c)")
-            if i == 0:
-                nc.sync.dma_start(out=out.rearrange("n (h a b) c -> h n a (b c)", h=2, a=8, b=P)[0], in_=flat)
+            src = acc[:, :, NB * c0 - w0 : NB * c1 - w0].rearrange("p j (c n) -> p c n j", n=NB)
+            dst = res[l][:, q, EDGE:].rearrange("p (c n j) -> p c n j", n=NB, j=4)
+            if l == 3:
+                nc.vector.tensor_copy(out=dst, in_=src)
             else:
-                nc.sync.dma_start(
-                    out=out.rearrange("n (r a b) c -> r n a (b c)", r=4, a=4, b=P)[i + 1], in_=flat[i - 1 : P : 2, :]
+                nc.scalar.copy(out=dst, in_=src)
+
+        def turn(bank, c, q):
+            l = 3 if c >= 9 else 2 if c >= 4 else 1
+            flat = res[l][:].rearrange("p q w -> p (q w)")
+            first = q * (EDGE + 64 * (2 * l + 1)) + 64 * (c - l * l)
+            nc.tensor.transpose(out=bank[:, c % 4, :], in_=flat[:, first : first + P], identity=ident[:])
+
+        def empty(bank, quad, q, engine):
+            src = bank[:].rearrange("p q o -> p o q")
+            dst = fins[q][:, :, 4 * quad : 4 * quad + 4]
+            if engine == "vector":
+                nc.vector.tensor_copy(out=dst, in_=src)
+            else:
+                nc.scalar.copy(out=dst, in_=src)
+
+        def four(quad, q, engine):
+            bank = psum_tr.tile([P, 4, P], F32, name="tr")
+            for c in range(4 * quad, 4 * quad + 4):
+                turn(bank, c, q)
+            empty(bank, quad, q, engine)
+
+        firsts = []
+
+        def first_three(q):
+            bank = psum_tr.tile([P, 4, P], F32, name="tr")
+            firsts.append(bank)
+            for c in range(1, 4):
+                turn(bank, c, q)
+
+        def direct(q, g):
+            for a in range(4):
+                ot = 4 * q + a
+                nc.tensor.matmul_mx(
+                    out=firsts[q][:, 0, :],
+                    lhsT=mask_codes[:, g, a, :].bitcast(FP8X4),
+                    lhsT_scale=mask_scales[:, g, a, :],
+                    rhs=wt[(0, g, ot)].bitcast(FP8X4),
+                    rhs_scale=planes[4 * g : P, 0, P * ot : P * (ot + 1)],
+                    start=(g == 0 and a == 0),
+                    stop=(g == G - 1 and a == 3),
                 )
 
-        passes(3, 0)
-        passes(3, 1)
-        finish(3, 0)
-        finish(3, 1)
+        def store(q, engine):
+            empty(firsts[q], 0, q, engine)
+            nc.sync.dma_start(
+                out=out[:, 4 * P * q : 4 * P * (q + 1), :].rearrange("n (a b) c -> n a (b c)", b=P),
+                in_=fins[q][EDGE : EDGE + 64].rearrange("p o c -> p (o c)"),
+            )
+
+        for q in range(Q):
+            passes(3, q)
+        for q in range(Q):
+            four(3, q, "vector")
         build_masks()
-        passes(2, 0)
-        passes(2, 1)
-        finish(2, 0)
-        passes(1, 0)
-        finish(2, 1)
-        passes(1, 1)
-        finish(1, 0)
-        direct(0, True)
-        direct(1, False)
-        direct(2, False)
+        for q in range(Q):
+            passes(2, q)
+        for half in range(2):
+            for q in (2 * half, 2 * half + 1):
+                four(2, q, "vector")
+                four(1, q, "scalar")
+            for q in (2 * half, 2 * half + 1):
+                passes(1, q)
+        first_three(0)
+        first_three(1)
+        for g in range(G):
+            direct(0, g)
+            direct(1, g)
+            if g == 0:
+                first_three(2)
+                first_three(3)
+        store(0, "scalar")
+        store(1, "vector")
+        for q in (2, 3):
+            for g in range(G):
+                direct(q, g)
+            store(q, "scalar")

@@ -17,7 +17,13 @@ G = 4
 FLOPS = 2 * NB * CH * 2048 * 2048
 
 WINDOW = {1: 0, 2: 64, 3: 128}
-PIECES = {3: ((0, 2048),), 2: ((0, 2048),), 1: ((0, 1024), (1024, 1024)), 0: ((0, 1024), (1024, 512), (1536, 512))}
+ALL = (0, 1, 2, 3)
+PIECES = {
+    3: ((0, 2048, ALL),),
+    2: ((0, 2048, ALL),),
+    1: ((0, 2048, ALL),),
+    0: ((0, 2048, (0,)), (0, 1024, (1, 2, 3)), (1024, 1024, (1,)), (1024, 512, (2, 3)), (1536, 512, (2, 3))),
+}
 Q = 4
 EDGE = 32
 DIAG = 516
@@ -64,8 +70,8 @@ def tile_irrepsstridelinear_w_kernel(
 
         wt = {}
         for l in degrees:
-            for first, width in PIECES[l]:
-                for g in range(G):
+            for first, width, gs in PIECES[l]:
+                for g in gs:
                     w_tile = keep.tile([P, width], U32, name="w%d_%d_%d" % (l, first, g), align_bytes=64)
                     nc.sync.dma_start(
                         out=w_tile[:].bitcast(I32),
@@ -120,9 +126,37 @@ def tile_irrepsstridelinear_w_kernel(
                     in_=diag[:, 0:2048],
                 )
 
-        def passes(l, q):
+        def take(acc, l, q, engine):
             c0 = l * l
             c1 = (l + 1) * (l + 1)
+            src = acc[:, :, NB * c0 - WINDOW[l] : NB * c1 - WINDOW[l]].rearrange("p j (c n) -> p c n j", n=NB)
+            dst = res[l][:, q, EDGE:].rearrange("p (c n j) -> p c n j", n=NB, j=4)
+            if engine == "vector":
+                nc.vector.tensor_copy(out=dst, in_=src)
+            else:
+                nc.scalar.copy(out=dst, in_=src)
+
+        accs = []
+
+        def sweep(g):
+            for q in range(Q):
+                if g == 0:
+                    accs.append(psum_acc.tile([P, 4, P], F32, name="acc"))
+                for j in range(4):
+                    ot = 4 * q + j
+                    nc.tensor.matmul_mx(
+                        out=accs[q][:, j, :],
+                        lhsT=wt[(1, g, ot)].bitcast(FP8X4),
+                        lhsT_scale=planes[4 * g : P, 1, P * ot : P * (ot + 1)],
+                        rhs=x_codes[:, g, WINDOW[1] : WINDOW[1] + P].bitcast(FP8X4),
+                        rhs_scale=x_scales[:, g, WINDOW[1] : WINDOW[1] + P],
+                        start=(g == 0 and j == 0),
+                        stop=(g == G - 1 and j == 3),
+                    )
+                if g == G - 1:
+                    take(accs[q], 1, q, "vector" if q % 2 == 0 else "scalar")
+
+        def passes(l, q):
             w0 = WINDOW[l]
             acc = psum_acc.tile([P, 4, P], F32, name="acc")
             for j in range(4):
@@ -137,12 +171,7 @@ def tile_irrepsstridelinear_w_kernel(
                         start=(g == 0),
                         stop=(g == G - 1),
                     )
-            src = acc[:, :, NB * c0 - w0 : NB * c1 - w0].rearrange("p j (c n) -> p c n j", n=NB)
-            dst = res[l][:, q, EDGE:].rearrange("p (c n j) -> p c n j", n=NB, j=4)
-            if l == 3:
-                nc.vector.tensor_copy(out=dst, in_=src)
-            else:
-                nc.scalar.copy(out=dst, in_=src)
+            take(acc, l, q, "vector" if l == 3 else "scalar")
 
         def turn(bank, c, q):
             l = 3 if c >= 9 else 2 if c >= 4 else 1
@@ -199,23 +228,22 @@ def tile_irrepsstridelinear_w_kernel(
         build_masks()
         for q in range(Q):
             passes(2, q)
-        for half in range(2):
-            for q in (2 * half, 2 * half + 1):
-                four(2, q, "vector")
-                four(1, q, "scalar")
-            for q in (2 * half, 2 * half + 1):
-                passes(1, q)
-        first_three(0)
-        first_three(1)
         for g in range(G):
+            four(2, g, "vector")
+            four(1, g, "scalar")
+            sweep(g)
+        for q in range(Q):
+            first_three(q)
+        for q in range(Q):
+            direct(q, 0)
+        for g in (1, 2, 3):
             direct(0, g)
             direct(1, g)
-            if g == 0:
-                first_three(2)
-                first_three(3)
         store(0, "scalar")
         store(1, "vector")
+        direct(2, 1)
+        direct(3, 1)
         for q in (2, 3):
-            for g in range(G):
+            for g in (2, 3):
                 direct(q, g)
             store(q, "scalar")

@@ -113,18 +113,17 @@ def tile_irrepsstridelinear_w_kernel(
         mask_codes = keep.tile([P, G, 4, P], U32, name="mask_codes", tag="rows_then_masks", align_bytes=64)
         mask_scales = keep.tile([P, G, 4, P], U8, align_bytes=64)
 
-        def build_masks():
+        def build_masks(g):
             spots = diag[:].rearrange("p (a r) -> p a r", r=DIAG)[:, :, 4 * EDGE : 4 * EDGE + 256]
             spots = spots.rearrange("p a (n s) -> p a n s", s=16)[:, :, :, 0:4]
-            for g in range(G):
-                nc.vector.tensor_copy(
-                    out=spots, in_=grouped[:, g, 0, :, :].unsqueeze(1).to_broadcast([P, 4, NB, 4])
-                )
-                nc.vector.quantize_mx(
-                    out=mask_codes[:, g].rearrange("p a j -> p (a j)").bitcast(FP8X4),
-                    scales=mask_scales[:, g].rearrange("p a j -> p (a j)"),
-                    in_=diag[:, 0:2048],
-                )
+            nc.vector.tensor_copy(
+                out=spots, in_=grouped[:, g, 0, :, :].unsqueeze(1).to_broadcast([P, 4, NB, 4])
+            )
+            nc.vector.quantize_mx(
+                out=mask_codes[:, g].rearrange("p a j -> p (a j)").bitcast(FP8X4),
+                scales=mask_scales[:, g].rearrange("p a j -> p (a j)"),
+                in_=diag[:, 0:2048],
+            )
 
         def take(acc, l, q, engine):
             c0 = l * l
@@ -136,25 +135,26 @@ def tile_irrepsstridelinear_w_kernel(
             else:
                 nc.scalar.copy(out=dst, in_=src)
 
-        accs = []
+        accs = {}
 
-        def sweep(g):
+        def sweep(l, g):
+            w0 = WINDOW[l]
             for q in range(Q):
                 if g == 0:
-                    accs.append(psum_acc.tile([P, 4, P], F32, name="acc"))
+                    accs[(l, q)] = psum_acc.tile([P, 4, P], F32, name="acc")
                 for j in range(4):
                     ot = 4 * q + j
                     nc.tensor.matmul_mx(
-                        out=accs[q][:, j, :],
-                        lhsT=wt[(1, g, ot)].bitcast(FP8X4),
-                        lhsT_scale=planes[4 * g : P, 1, P * ot : P * (ot + 1)],
-                        rhs=x_codes[:, g, WINDOW[1] : WINDOW[1] + P].bitcast(FP8X4),
-                        rhs_scale=x_scales[:, g, WINDOW[1] : WINDOW[1] + P],
+                        out=accs[(l, q)][:, j, :],
+                        lhsT=wt[(l, g, ot)].bitcast(FP8X4),
+                        lhsT_scale=planes[4 * g : P, l, P * ot : P * (ot + 1)],
+                        rhs=x_codes[:, g, w0 : w0 + P].bitcast(FP8X4),
+                        rhs_scale=x_scales[:, g, w0 : w0 + P],
                         start=(g == 0 and j == 0),
                         stop=(g == G - 1 and j == 3),
                     )
                 if g == G - 1:
-                    take(accs[q], 1, q, "vector" if q % 2 == 0 else "scalar")
+                    take(accs[(l, q)], l, q, "vector" if q % 2 == 0 else "scalar")
 
         def passes(l, q):
             w0 = WINDOW[l]
@@ -171,7 +171,7 @@ def tile_irrepsstridelinear_w_kernel(
                         start=(g == 0),
                         stop=(g == G - 1),
                     )
-            take(acc, l, q, "vector" if l == 3 else "scalar")
+            take(acc, l, q, "vector")
 
         def turn(bank, c, q):
             l = 3 if c >= 9 else 2 if c >= 4 else 1
@@ -223,15 +223,19 @@ def tile_irrepsstridelinear_w_kernel(
 
         for q in range(Q):
             passes(3, q)
-        for q in range(Q):
-            four(3, q, "vector")
-        build_masks()
-        for q in range(Q):
-            passes(2, q)
+        sweep(2, 0)
+        four(3, 0, "scalar")
+        four(3, 1, "vector")
+        sweep(2, 1)
+        four(3, 2, "scalar")
+        four(3, 3, "vector")
+        sweep(2, 2)
+        sweep(2, 3)
         for g in range(G):
             four(2, g, "vector")
             four(1, g, "scalar")
-            sweep(g)
+            build_masks(g)
+            sweep(1, g)
         for q in range(Q):
             first_three(q)
         for q in range(Q):

@@ -47,8 +47,11 @@ def tile_irrepsstridelinear_w_kernel(
         nc.sync.dma_start(out=rows[32:96, :], in_=x.rearrange("n (g q) c -> (n g) (q c)", g=G))
 
         planes = keep.tile([P, 4, 2048], U8, align_bytes=64)
+        zero = keep.tile([P, 1], F32)
+        nc.vector.memset(zero[:], 0.0)
         for l in degrees:
             nc.vector.memset(planes[:, l, :].bitcast(I32), 0)
+        nc.scalar.copy(out=rows[96:128, 0:4096].bitcast(F32), in_=zero[96:128, 0:1].to_broadcast([32, 2048]))
         for q in range(4):
             nc.scalar.dma_start(
                 out=planes[32 * q : 32 * q + 16, 3, :].bitcast(F32),
@@ -58,7 +61,7 @@ def tile_irrepsstridelinear_w_kernel(
         ident = keep.tile([P, P], F32)
         make_identity(nc, ident[:])
         nc.vector.memset(rows[0:32, :].bitcast(I32), 0)
-        nc.gpsimd.memset(rows[96:128, :].bitcast(F32), 0.0)
+        nc.vector.memset(rows[96:128, 4096:8192].bitcast(I32), 0)
         for l in (2, 1, 0):
             for q in range(4):
                 nc.gpsimd.dma_start(
@@ -84,8 +87,8 @@ def tile_irrepsstridelinear_w_kernel(
         x_codes = keep.tile([P, G, CH * NB], U32, align_bytes=64)
         x_scales = keep.tile([P, G, CH * NB], U8, align_bytes=64)
         row_words = rows[:].bitcast(F32)
-        for d in range(CH // 2):
-            if d % 2 == 0:
+        def turn_x(d):
+            if d >= 4:
                 bank = psum_acc.tile([P, 4, P], F32, name="acc")
             else:
                 bank = psum_tr.tile([P, 4, P], F32, name="tr")
@@ -98,12 +101,17 @@ def tile_irrepsstridelinear_w_kernel(
                     nc.vector.tensor_copy(out=grouped[:, :, 2 * d + e, :, :], in_=src)
                 else:
                     nc.scalar.copy(out=grouped[:, :, 2 * d + e, :, :], in_=src)
-        for g in range(G):
-            nc.vector.quantize_mx(
-                out=x_codes[:, g, :].bitcast(FP8X4),
-                scales=x_scales[:, g, :],
-                in_=grouped[:, g].rearrange("p c n t -> p (c n t)"),
-            )
+
+        for half in (1, 0):
+            for d in range(4 * half, 4 * half + 4):
+                turn_x(d)
+            for g in range(G):
+                cols = slice(P * half, P * (half + 1))
+                nc.vector.quantize_mx(
+                    out=x_codes[:, g, cols].bitcast(FP8X4),
+                    scales=x_scales[:, g, cols],
+                    in_=grouped[:, g, 8 * half : 8 * half + 8].rearrange("p c n t -> p (c n t)"),
+                )
 
         res = {}
         for l in (3, 2, 1):
@@ -141,7 +149,10 @@ def tile_irrepsstridelinear_w_kernel(
             w0 = WINDOW[l]
             for q in range(Q):
                 if g == 0:
-                    accs[(l, q)] = psum_acc.tile([P, 4, P], F32, name="acc")
+                    if l == 2:
+                        accs[(l, q)] = psum_tr.tile([P, 4, P], F32, name="tr")
+                    else:
+                        accs[(l, q)] = psum_acc.tile([P, 4, P], F32, name="acc")
                 for j in range(4):
                     ot = 4 * q + j
                     nc.tensor.matmul_mx(
@@ -155,23 +166,6 @@ def tile_irrepsstridelinear_w_kernel(
                     )
                 if g == G - 1:
                     take(accs[(l, q)], l, q, "vector" if q % 2 == 0 else "scalar")
-
-        def passes(l, q):
-            w0 = WINDOW[l]
-            acc = psum_acc.tile([P, 4, P], F32, name="acc")
-            for j in range(4):
-                ot = 4 * q + j
-                for g in range(G):
-                    nc.tensor.matmul_mx(
-                        out=acc[:, j, :],
-                        lhsT=wt[(l, g, ot)].bitcast(FP8X4),
-                        lhsT_scale=planes[4 * g : P, l, P * ot : P * (ot + 1)],
-                        rhs=x_codes[:, g, w0 : w0 + P].bitcast(FP8X4),
-                        rhs_scale=x_scales[:, g, w0 : w0 + P],
-                        start=(g == 0),
-                        stop=(g == G - 1),
-                    )
-            take(acc, l, q, "vector")
 
         def turn(bank, c, q):
             l = 3 if c >= 9 else 2 if c >= 4 else 1
@@ -187,11 +181,15 @@ def tile_irrepsstridelinear_w_kernel(
             else:
                 nc.scalar.copy(out=dst, in_=src)
 
-        def four(quad, q, engine):
-            bank = psum_tr.tile([P, 4, P], F32, name="tr")
-            for c in range(4 * quad, 4 * quad + 4):
-                turn(bank, c, q)
-            empty(bank, quad, q, engine)
+        def fours(quad):
+            for q in range(Q):
+                if quad != 2:
+                    bank = psum_acc.tile([P, 4, P], F32, name="acc")
+                else:
+                    bank = psum_tr.tile([P, 4, P], F32, name="tr")
+                for c in range(4 * quad, 4 * quad + 4):
+                    turn(bank, c, q)
+                empty(bank, quad, q, "vector" if q % 2 == 0 else "scalar")
 
         firsts = []
 
@@ -221,32 +219,33 @@ def tile_irrepsstridelinear_w_kernel(
                 in_=fins[q][EDGE : EDGE + 64].rearrange("p o c -> p (o c)"),
             )
 
-        for q in range(Q):
-            passes(3, q)
+        for g in range(G):
+            sweep(3, g)
         sweep(2, 0)
-        four(3, 0, "scalar")
-        four(3, 1, "vector")
         sweep(2, 1)
-        four(3, 2, "scalar")
-        four(3, 3, "vector")
+        fours(3)
+        build_masks(0)
+        build_masks(1)
         sweep(2, 2)
         sweep(2, 3)
+        fours(2)
+        fours(1)
+        build_masks(2)
+        build_masks(3)
         for g in range(G):
-            four(2, g, "vector")
-            four(1, g, "scalar")
-            build_masks(g)
             sweep(1, g)
-        for q in range(Q):
-            first_three(q)
-        for q in range(Q):
-            direct(q, 0)
-        for g in (1, 2, 3):
+        first_three(0)
+        first_three(1)
+        for g in range(G):
             direct(0, g)
             direct(1, g)
         store(0, "scalar")
         store(1, "vector")
-        direct(2, 1)
-        direct(3, 1)
+        first_three(2)
+        first_three(3)
+        for g in (0, 1):
+            direct(2, g)
+            direct(3, g)
         for q in (2, 3):
             for g in (2, 3):
                 direct(q, g)

from contextlib import ExitStack

import concourse.mybir as mybir
from concourse.masks import make_identity

F32 = mybir.dt.float32
BF16 = mybir.dt.bfloat16
I32 = mybir.dt.int32
U32 = mybir.dt.uint32
U8 = mybir.dt.uint8
FP8X4 = mybir.dt.float8_e4m3fn_x4

P = 128
NB = 16
CH = 16
G = 4
FLOPS = 2 * NB * CH * 2048 * 2048

WINDOW = {1: 0, 2: 64, 3: 128}
ALL = (0, 1, 2, 3)
PIECES = {
    3: ((0, 2048, ALL),),
    2: ((0, 2048, ALL),),
    1: ((0, 2048, ALL),),
    0: ((0, 2048, (0,)), (0, 1024, (1, 2, 3)), (1024, 1024, (1,)), (1024, 512, (2, 3)), (1536, 512, (2, 3))),
}
Q = 4
EDGE = 32
DIAG = 516


def tile_irrepsstridelinear_w_kernel(
    tc, x, w0_words, w0_scales, w1_words, w1_scales, w2_words, w2_scales, w3_words, w3_scales, out
):
    nc = tc.nc
    words = (w0_words, w1_words, w2_words, w3_words)
    scales = (w0_scales, w1_scales, w2_scales, w3_scales)
    degrees = (3, 2, 1, 0)

    with ExitStack() as ctx:
        keep = ctx.enter_context(tc.tile_pool(name="keep", bufs=1))
        psum_acc = ctx.enter_context(tc.psum_pool(name="acc", bufs=4))
        psum_tr = ctx.enter_context(tc.psum_pool(name="tr", bufs=4))
        ctx.enter_context(tc.manual_schedule())

        rows = keep.tile([P, 8192], BF16, name="rows", tag="rows_then_masks", align_bytes=64)
        nc.sync.dma_start(out=rows[32:96, :], in_=x.rearrange("n (g q) c -> (n g) (q c)", g=G))

        planes = keep.tile([P, 4, 2048], U8, align_bytes=64)
        zero = keep.tile([P, 1], F32)
        nc.vector.memset(zero[:], 0.0)
        for l in degrees:
            nc.vector.memset(planes[:, l, :].bitcast(I32), 0)
        nc.scalar.copy(out=rows[96:128, 0:4096].bitcast(F32), in_=zero[96:128, 0:1].to_broadcast([32, 2048]))
        for q in range(4):
            nc.scalar.dma_start(
                out=planes[32 * q : 32 * q + 16, 3, :].bitcast(F32),
                in_=scales[3][:, 4 * q : 4 * q + 4, :].bitcast(F32),
            )

        ident = keep.tile([P, P], F32)
        make_identity(nc, ident[:])
        nc.vector.memset(rows[0:32, :].bitcast(I32), 0)
        nc.vector.memset(rows[96:128, 4096:8192].bitcast(I32), 0)
        for l in (2, 1, 0):
            for q in range(4):
                nc.gpsimd.dma_start(
                    out=planes[32 * q : 32 * q + 16, l, :].bitcast(F32),
                    in_=scales[l][:, 4 * q : 4 * q + 4, :].bitcast(F32),
                )
        diag = keep.tile([P, 4 * DIAG], BF16, align_bytes=64)
        nc.vector.memset(diag[:].bitcast(I32), 0)

        wt = {}
        for l in degrees:
            for first, width, gs in PIECES[l]:
                for g in gs:
                    w_tile = keep.tile([P, width], U32, name="w%d_%d_%d" % (l, first, g), align_bytes=64)
                    nc.sync.dma_start(
                        out=w_tile[:].bitcast(I32),
                        in_=words[l][g].rearrange("p n t -> p (n t)")[:, 4 * first : 4 * (first + width)].bitcast(I32),
                    )
                    for ot in range(first // P, (first + width) // P):
                        wt[(l, g, ot)] = w_tile[:, P * ot - first : P * (ot + 1) - first]

        grouped = keep.tile([P, G, CH, NB, 4], BF16, align_bytes=64)
        x_codes = keep.tile([P, G, CH * NB], U32, align_bytes=64)
        x_scales = keep.tile([P, G, CH * NB], U8, align_bytes=64)
        row_words = rows[:].bitcast(F32)
        def turn_x(d):
            if d >= 4:
                bank = psum_acc.tile([P, 4, P], F32, name="acc")
            else:
                bank = psum_tr.tile([P, 4, P], F32, name="tr")
            for t in range(4):
                nc.tensor.transpose(out=bank[:, t, :], in_=row_words[:, 8 * t + d : 4096 : 32], identity=ident[:])
            halves = bank[:].bitcast(BF16).rearrange("p t (s e) -> p t s e", e=2)
            for e in range(2):
                src = halves[:, :, 32:96, e].rearrange("p t (n g) -> p g n t", g=G)
                if d % 2 == 0:
                    nc.vector.tensor_copy(out=grouped[:, :, 2 * d + e, :, :], in_=src)
                else:
                    nc.scalar.copy(out=grouped[:, :, 2 * d + e, :, :], in_=src)

        for half in (1, 0):
            for d in range(4 * half, 4 * half + 4):
                turn_x(d)
            for g in range(G):
                cols = slice(P * half, P * (half + 1))
                nc.vector.quantize_mx(
                    out=x_codes[:, g, cols].bitcast(FP8X4),
                    scales=x_scales[:, g, cols],
                    in_=grouped[:, g, 8 * half : 8 * half + 8].rearrange("p c n t -> p (c n t)"),
                )

        res = {}
        for l in (3, 2, 1):
            res[l] = keep.tile([P, Q + 1, EDGE + 64 * (2 * l + 1)], F32, name="res%d" % l)
            nc.vector.memset(res[l][:, :, 0:EDGE], 0.0)
        fins = [keep.tile([P, P, CH], F32, name="fin%d" % i) for i in range(Q)]
        mask_codes = keep.tile([P, G, 4, P], U32, name="mask_codes", tag="rows_then_masks", align_bytes=64)
        mask_scales = keep.tile([P, G, 4, P], U8, align_bytes=64)

        def build_masks(g):
            spots = diag[:].rearrange("p (a r) -> p a r", r=DIAG)[:, :, 4 * EDGE : 4 * EDGE + 256]
            spots = spots.rearrange("p a (n s) -> p a n s", s=16)[:, :, :, 0:4]
            nc.vector.tensor_copy(
                out=spots, in_=grouped[:, g, 0, :, :].unsqueeze(1).to_broadcast([P, 4, NB, 4])
            )
            nc.vector.quantize_mx(
                out=mask_codes[:, g].rearrange("p a j -> p (a j)").bitcast(FP8X4),
                scales=mask_scales[:, g].rearrange("p a j -> p (a j)"),
                in_=diag[:, 0:2048],
            )

        def take(acc, l, q, engine):
            c0 = l * l
            c1 = (l + 1) * (l + 1)
            src = acc[:, :, NB * c0 - WINDOW[l] : NB * c1 - WINDOW[l]].rearrange("p j (c n) -> p c n j", n=NB)
            dst = res[l][:, q, EDGE:].rearrange("p (c n j) -> p c n j", n=NB, j=4)
            if engine == "vector":
                nc.vector.tensor_copy(out=dst, in_=src)
            else:
                nc.scalar.copy(out=dst, in_=src)

        accs = {}

        def sweep(l, g):
            w0 = WINDOW[l]
            for q in range(Q):
                if g == 0:
                    if l == 2:
                        accs[(l, q)] = psum_tr.tile([P, 4, P], F32, name="tr")
                    else:
                        accs[(l, q)] = psum_acc.tile([P, 4, P], F32, name="acc")
                for j in range(4):
                    ot = 4 * q + j
                    nc.tensor.matmul_mx(
                        out=accs[(l, q)][:, j, :],
                        lhsT=wt[(l, g, ot)].bitcast(FP8X4),
                        lhsT_scale=planes[4 * g : P, l, P * ot : P * (ot + 1)],
                        rhs=x_codes[:, g, w0 : w0 + P].bitcast(FP8X4),
                        rhs_scale=x_scales[:, g, w0 : w0 + P],
                        start=(g == 0 and j == 0),
                        stop=(g == G - 1 and j == 3),
                    )
                if g == G - 1:
                    take(accs[(l, q)], l, q, "vector" if q % 2 == 0 else "scalar")

        def turn(bank, c, q):
            l = 3 if c >= 9 else 2 if c >= 4 else 1
            flat = res[l][:].rearrange("p q w -> p (q w)")
            first = q * (EDGE + 64 * (2 * l + 1)) + 64 * (c - l * l)
            nc.tensor.transpose(out=bank[:, c % 4, :], in_=flat[:, first : first + P], identity=ident[:])

        def empty(bank, quad, q, engine):
            src = bank[:].rearrange("p q o -> p o q")
            dst = fins[q][:, :, 4 * quad : 4 * quad + 4]
            if engine == "vector":
                nc.vector.tensor_copy(out=dst, in_=src)
            else:
                nc.scalar.copy(out=dst, in_=src)

        def fours(quad):
            for q in range(Q):
                if quad != 2:
                    bank = psum_acc.tile([P, 4, P], F32, name="acc")
                else:
                    bank = psum_tr.tile([P, 4, P], F32, name="tr")
                for c in range(4 * quad, 4 * quad + 4):
                    turn(bank, c, q)
                empty(bank, quad, q, "vector" if q % 2 == 0 else "scalar")

        firsts = []

        def first_three(q):
            bank = psum_tr.tile([P, 4, P], F32, name="tr")
            firsts.append(bank)
            for c in range(1, 4):
                turn(bank, c, q)

        def direct(q, g):
            for a in range(4):
                ot = 4 * q + a
                nc.tensor.matmul_mx(
                    out=firsts[q][:, 0, :],
                    lhsT=mask_codes[:, g, a, :].bitcast(FP8X4),
                    lhsT_scale=mask_scales[:, g, a, :],
                    rhs=wt[(0, g, ot)].bitcast(FP8X4),
                    rhs_scale=planes[4 * g : P, 0, P * ot : P * (ot + 1)],
                    start=(g == 0 and a == 0),
                    stop=(g == G - 1 and a == 3),
                )

        def store(q, engine):
            empty(firsts[q], 0, q, engine)
            nc.sync.dma_start(
                out=out[:, 4 * P * q : 4 * P * (q + 1), :].rearrange("n (a b) c -> n a (b c)", b=P),
                in_=fins[q][EDGE : EDGE + 64].rearrange("p o c -> p (o c)"),
            )

        for g in range(G):
            sweep(3, g)
        sweep(2, 0)
        sweep(2, 1)
        fours(3)
        build_masks(0)
        build_masks(1)
        sweep(2, 2)
        sweep(2, 3)
        fours(2)
        fours(1)
        build_masks(2)
        build_masks(3)
        for g in range(G):
            sweep(1, g)
        first_three(0)
        first_three(1)
        for g in range(G):
            direct(0, g)
            direct(1, g)
        store(0, "scalar")
        store(1, "vector")
        first_three(2)
        first_three(3)
        for g in (0, 1):
            direct(2, g)
            direct(3, g)
        for q in (2, 3):
            for g in (2, 3):
                direct(q, g)
            store(q, "scalar")
